import numpy as np
import ml_dtypes


def mxq(x, axis, fmt="e4m3"):
    dtype, down = {"e4m3": (ml_dtypes.float8_e4m3fn, 7), "e5m2": (ml_dtypes.float8_e5m2, 14)}[fmt]
    v = np.moveaxis(np.asarray(x, np.float32).astype(ml_dtypes.bfloat16).astype(np.float64), axis, -1)
    blocks = v.reshape(v.shape[:-1] + (-1, 32))
    amax = np.abs(blocks).max(-1, keepdims=True)
    byte = np.maximum(np.where(amax > 0, np.frexp(amax)[1] - 1 + 127, 0) - down, 1)
    scale = np.exp2(byte - 127.0)
    codes = (blocks / scale).astype(np.float32).astype(dtype).astype(np.float64)
    return np.moveaxis((codes * scale).reshape(v.shape), -1, axis)


WIDE = False


def mx_kscale(k):
    if not WIDE:
        return np.ones(k)
    levels = np.array([10, -10, 5, -5, 0])
    if k % 512:
        return np.exp2(np.random.permutation(np.resize(levels, k // 32))).repeat(32)
    a = np.empty((k // 512, 16))
    for p in range(k // 512):
        a[p, :8] = np.random.permutation(np.resize(levels, 8))
        for g in range(8):
            far = levels[np.abs(levels - a[p, g]) >= 10]
            a[p, g + 8] = far[np.random.randint(len(far))]
    return np.exp2(a.ravel()).repeat(32)


BF16 = ml_dtypes.bfloat16


def bf(x):
    return np.asarray(x, np.float32).astype(BF16)


def f64(x):
    return np.asarray(x).astype(np.float64)


B, D, MP, MID, L = 4096, 768, 512, 1024, 4
HALF = D // 2


def setup_inputs():
    s = mx_kscale(MP)
    t = mx_kscale(MID)
    return {
        "x": bf(np.random.standard_normal((B, D))),
        "h_prev": bf(np.maximum(np.random.standard_normal((B, MP)) * np.sqrt(2.0), 0.0) * s),
        "w_hid": bf(np.random.standard_normal((MP, MID)) * np.sqrt(2.0 / MP) / s[:, None] * t),
        "b_hid": bf(np.random.standard_normal(MID) * 0.2 * t),
        "w_out": bf(np.random.standard_normal((MID, HALF)) / np.sqrt(MID) / t[:, None]),
        "b_out": bf(np.random.standard_normal(HALF) * 0.2),
    }


def reference(x, h_prev, w_hid, b_hid, w_out, b_out):
    x = f64(x)
    first = x[:, 0::2]
    second = x[:, 1::2]
    h = np.maximum((mxq(f64(h_prev), 1, "e4m3") @ mxq(f64(w_hid), 0, "e4m3")) + f64(b_hid), 0.0)
    shift = (mxq(h, 1, "e4m3") @ mxq(f64(w_out), 0, "e4m3")) + f64(b_out)
    y_second = second + shift
    return np.stack([first, y_second], axis=2).reshape(x.shape)

@@ -1,0 +1,267 @@
+import concourse.mybir as mybir
+from concourse.masks import make_identity
+
+F32 = mybir.dt.float32
+BF16 = mybir.dt.bfloat16
+U32 = mybir.dt.uint32
+U8 = mybir.dt.uint8
+FP8X4 = mybir.dt.float8_e4m3fn_x4
+ADD = mybir.AluOpType.add
+RELU = mybir.ActivationFunctionType.Relu
+
+P = 128
+PACK = 4
+K_PASS = P * PACK
+
+TOKENS, D, MP, MID = 4096, 768, 512, 1024
+HALF = D // 2
+GROUP = 512
+TILES = GROUP // P
+N_GROUPS = TOKENS // GROUP
+MID_PASSES = MID // K_PASS
+OUT_PIECES = ((0, 256), (256, 384))
+
+LAG = 2
+
+FLOPS = 2 * TOKENS * (MP * MID + MID * HALF)
+
+
+def tile_additivecoupling_pa_t_kernel(tc, x, h_prev, w_hid, b_hid, w_out, b_out, out):
+    nc = tc.nc
+
+    def token_rows(dram, i):
+        return dram[i * GROUP : (i + 1) * GROUP, :].rearrange("(p t) c -> p (t c)", t=TILES)
+
+    with tc.manual_schedule(), tc.tile_pool(name="consts", bufs=1) as consts, tc.tile_pool(
+        name="inputs", bufs=1
+    ) as inputs, tc.tile_pool(name="work", bufs=3) as work, tc.psum_pool(
+        name="psum_t", bufs=2
+    ) as psum_t, tc.psum_pool(name="psum_h", bufs=4) as psum_h, tc.psum_pool(
+        name="psum_s", bufs=2
+    ) as psum_s:
+        hp_tiles = []
+        x_tiles = []
+        for i in range(N_GROUPS):
+            hp_sb = inputs.tile([P, TILES * MP], BF16, name="hp%d" % i)
+            hp_tiles.append(hp_sb)
+            x_sb = inputs.tile([P, TILES * D], BF16, name="x%d" % i)
+            x_tiles.append(x_sb)
+        nc.sync.dma_start(out=hp_tiles[0][:], in_=token_rows(h_prev, 0))
+        whid_raw = consts.tile([P, PACK, MID], BF16)
+        for g in range(MID_PASSES):
+            cols = slice(g * K_PASS, (g + 1) * K_PASS)
+            nc.sync.dma_start(
+                out=whid_raw[:, :, cols], in_=w_hid[:, cols].rearrange("(q j) n -> q j n", j=PACK)
+            )
+        nc.sync.dma_start(out=hp_tiles[1][:], in_=token_rows(h_prev, 1))
+        wout_raw = consts.tile([P, MID_PASSES, PACK, HALF], BF16)
+        nc.sync.dma_start(
+            out=wout_raw[:], in_=w_out.rearrange("(g p j) n -> p g j n", g=MID_PASSES, j=PACK)
+        )
+        bout = consts.tile([P, HALF], BF16)
+        for i in range(N_GROUPS):
+            if i + 2 < N_GROUPS:
+                nc.sync.dma_start(out=hp_tiles[i + 2][:], in_=token_rows(h_prev, i + 2))
+            nc.sync.dma_start(out=x_tiles[i][:], in_=token_rows(x, i))
+            if i == 0:
+                nc.sync.dma_start(out=bout[:], in_=b_out.partition_broadcast(P))
+
+        bhid_bf = consts.tile([P, MID_PASSES * PACK], BF16)
+        nc.scalar.dma_start(
+            out=bhid_bf[:].rearrange("p (g j) -> p g j", j=PACK),
+            in_=b_hid.rearrange("(g p j) -> p g j", g=MID_PASSES, j=PACK),
+        )
+
+        ident = consts.tile([P, P], F32)
+        make_identity(nc, ident[:])
+
+        shift_planes = []
+        for s in range(2):
+            planes_sb = consts.tile([P, TILES, 2, HALF], F32, name="shift_planes%d" % s)
+            nc.vector.memset(planes_sb[:, :, 0, :], 0.0)
+            shift_planes.append(planes_sb)
+        bhid = consts.tile([P, MID_PASSES * PACK], F32)
+        nc.vector.tensor_copy(out=bhid[:], in_=bhid_bf[:])
+
+        whid_grouped = consts.tile([P, MID, PACK], BF16, align_bytes=64)
+        whid_codes = consts.tile([P, MID], U32, align_bytes=64)
+        whid_scales = consts.tile([P, MID], U8, align_bytes=64)
+        wout_grouped = consts.tile([P, MID_PASSES, HALF, PACK], BF16, align_bytes=64)
+        wout_codes = consts.tile([P, MID_PASSES, HALF], U32, align_bytes=64)
+        wout_scales = consts.tile([P, MID_PASSES, HALF], U8, align_bytes=64)
+
+        def quantise_w_hid(g):
+            cols = slice(g * K_PASS, (g + 1) * K_PASS)
+            nc.vector.tensor_copy(
+                out=whid_grouped[:, cols, :].rearrange("q (j p) s -> q j p s", j=PACK),
+                in_=whid_raw[:, :, cols].rearrange("q s (p j) -> q j p s", j=PACK),
+            )
+            nc.vector.quantize_mx(
+                out=whid_codes[:, cols].bitcast(FP8X4),
+                scales=whid_scales[:, cols],
+                in_=whid_grouped[:, cols, :].rearrange("q c s -> q (c s)"),
+            )
+
+        def quantise_w_out():
+            for g in range(MID_PASSES):
+                nc.vector.tensor_copy(
+                    out=wout_grouped[:, g], in_=wout_raw[:, g].rearrange("p j n -> p n j")
+                )
+            for g in range(MID_PASSES):
+                for n0, n1 in OUT_PIECES:
+                    nc.vector.quantize_mx(
+                        out=wout_codes[:, g, n0:n1].bitcast(FP8X4),
+                        scales=wout_scales[:, g, n0:n1],
+                        in_=wout_grouped[:, g, n0:n1, :].rearrange("p n j -> p (n j)"),
+                    )
+
+        flipped = {}
+        hp_grouped = {}
+        hp_mx = {}
+        h_acc = {}
+        h_rows = {}
+        h_grouped = {}
+        h_mx = {}
+        shift_acc = {}
+
+        def transpose_h_prev(i):
+            hp_words = hp_tiles[i][:].bitcast(F32)
+            for b in range(TILES // 2):
+                flipped[i, b] = psum_t.tile([P, 2, 2 * P], F32, name="flipped")
+                for t2 in range(2):
+                    for u in range(2):
+                        row_words = (2 * b + t2) * 2 * P
+                        nc.tensor.transpose(
+                            flipped[i, b][:, u, t2 * P : (t2 + 1) * P],
+                            hp_words[:, row_words + u : row_words + 2 * P : 2],
+                            ident[:],
+                        )
+
+        def copy_h_prev(i):
+            hp_grouped[i] = work.tile(
+                [P, GROUP * PACK], BF16, align_bytes=64, bufs=2, name="hp_grouped"
+            )
+            grouped_words = hp_grouped[i][:].bitcast(F32).rearrange("q (c u) -> q c u", u=2)
+            for b in range(TILES // 2):
+                nc.scalar.copy(
+                    out=grouped_words[:, b * 2 * P : (b + 1) * 2 * P, :],
+                    in_=flipped[i, b][:].rearrange("q u c -> q c u"),
+                )
+
+        def quantise_h_prev(i):
+            hp_codes = work.tile([P, GROUP], U32, align_bytes=64)
+            hp_scales = work.tile([P, GROUP], U8, align_bytes=64)
+            nc.vector.quantize_mx(
+                out=hp_codes[:].bitcast(FP8X4), scales=hp_scales[:], in_=hp_grouped[i][:]
+            )
+            hp_mx[i] = (hp_codes, hp_scales)
+
+        def hidden_matmuls(i, g):
+            hp_codes, hp_scales = hp_mx[i]
+            for j in range(PACK):
+                m = g * PACK + j
+                h_acc[i, g, j] = psum_h.tile([P, GROUP], F32, name="h_acc")
+                nc.tensor.matmul_mx(
+                    out=h_acc[i, g, j][:],
+                    lhsT=whid_codes[:, m * P : (m + 1) * P].bitcast(FP8X4),
+                    lhsT_scale=whid_scales[:, m * P : (m + 1) * P],
+                    rhs=hp_codes[:].bitcast(FP8X4),
+                    rhs_scale=hp_scales[:],
+                    start=True,
+                    stop=True,
+                )
+
+        def hidden_relu(i, g):
+            h_rows[i, g] = work.tile([P, PACK, GROUP], BF16, name="h_rows")
+            for j in range(PACK):
+                m = g * PACK + j
+                nc.scalar.activation(
+                    out=h_rows[i, g][:, j, :], in_=h_acc[i, g, j][:], func=RELU, bias=bhid[:, m : m + 1]
+                )
+
+        def regroup_h(i, g):
+            copy = nc.scalar.copy if (g == 1 and i > 0) else nc.vector.tensor_copy
+            h_grouped[i, g] = work.tile([P, GROUP, PACK], BF16, align_bytes=64, name="h_grouped")
+            copy(
+                out=h_grouped[i, g][:].rearrange("p (c i) j -> p c j i", i=4),
+                in_=h_rows[i, g][:].rearrange("p j (c i) -> p c j i", i=4),
+            )
+
+        def quantise_h(i, g):
+            if g == 0:
+                h_codes = work.tile([P, MID_PASSES, GROUP], U32, align_bytes=64)
+                h_scales = work.tile([P, MID_PASSES, GROUP], U8, align_bytes=64)
+                h_mx[i] = (h_codes, h_scales)
+            h_codes, h_scales = h_mx[i]
+            nc.vector.quantize_mx(
+                out=h_codes[:, g, :].bitcast(FP8X4),
+                scales=h_scales[:, g, :],
+                in_=h_grouped[i, g][:].rearrange("p c j -> p (c j)"),
+            )
+
+        def shift_matmuls(i, pair):
+            h_codes, h_scales = h_mx[i]
+            for t in (2 * pair, 2 * pair + 1):
+                tokens = slice(t * P, (t + 1) * P)
+                shift_acc[i, t] = psum_s.tile([P, HALF], F32, name="shift_acc")
+                for n0, n1 in OUT_PIECES:
+                    for g in range(MID_PASSES):
+                        nc.tensor.matmul_mx(
+                            out=shift_acc[i, t][:, n0:n1],
+                            lhsT=h_codes[:, g, tokens].bitcast(FP8X4),
+                            lhsT_scale=h_scales[:, g, tokens],
+                            rhs=wout_codes[:, g, n0:n1].bitcast(FP8X4),
+                            rhs_scale=wout_scales[:, g, n0:n1],
+                            start=(g == 0),
+                            stop=(g == MID_PASSES - 1),
+                        )
+
+        def add_b_out(i, pair):
+            for t in (2 * pair, 2 * pair + 1):
+                nc.vector.tensor_tensor(
+                    out=shift_planes[i % 2][:, t, 1, :], in0=shift_acc[i, t][:], in1=bout[:], op=ADD
+                )
+
+        def add_to_x(i, pair):
+            tiles = slice(2 * pair, 2 * pair + 2)
+            y_sb = work.tile([P, 2, HALF, 2], F32)
+            nc.vector.tensor_tensor(
+                out=y_sb[:],
+                in0=x_tiles[i][:].rearrange("p (t c e) -> p t c e", t=TILES, e=2)[:, tiles],
+                in1=shift_planes[i % 2][:, tiles].rearrange("p t e c -> p t c e"),
+                op=ADD,
+            )
+            nc.sync.dma_start(
+                out=token_rows(out, i).rearrange("p (t c) -> p t c", t=TILES)[:, tiles],
+                in_=y_sb[:].rearrange("p t c e -> p t (c e)"),
+            )
+
+        def run(step, i, *args):
+            if 0 <= i < N_GROUPS:
+                step(i, *args)
+
+        transpose_h_prev(0)
+        copy_h_prev(0)
+        quantise_w_hid(0)
+        quantise_h_prev(0)
+        hidden_matmuls(0, 0)
+        quantise_w_hid(1)
+        quantise_w_out()
+        for i in range(N_GROUPS + LAG):
+            run(quantise_h, i - 1, 1)
+            run(transpose_h_prev, i + 1)
+            run(shift_matmuls, i - 1, 0)
+            run(hidden_relu, i, 0)
+            run(add_to_x, i - 2, 1)
+            run(add_b_out, i - 1, 0)
+            run(hidden_matmuls, i, 1)
+            run(copy_h_prev, i + 1)
+            run(regroup_h, i, 0)
+            run(quantise_h_prev, i + 1)
+            run(quantise_h, i, 0)
+            run(shift_matmuls, i - 1, 1)
+            run(hidden_relu, i, 1)
+            run(hidden_matmuls, i + 1, 0)
+            run(add_b_out, i - 1, 1)
+            run(add_to_x, i - 1, 0)
+            run(regroup_h, i, 1)

@@ -15,9 +15,10 @@ K_PASS = P * PACK
 
 TOKENS, D, MP, MID = 4096, 768, 512, 1024
 HALF = D // 2
-GROUP = 512
-TILES = GROUP // P
-N_GROUPS = TOKENS // GROUP
+MAX_GROUP = 512
+MAX_TILES = MAX_GROUP // P
+GROUPS = (256,) + 7 * (MAX_GROUP,) + (256,)
+N_GROUPS = len(GROUPS)
 MID_PASSES = MID // K_PASS
 OUT_PIECES = ((0, 256), (256, 384))
 
@@ -29,8 +30,12 @@ FLOPS = 2 * TOKENS * (MP * MID + MID * HALF)
 def tile_additivecoupling_pa_t_kernel(tc, x, h_prev, w_hid, b_hid, w_out, b_out, out):
     nc = tc.nc
 
+    def tiles_of(i):
+        return GROUPS[i] // P
+
     def token_rows(dram, i):
-        return dram[i * GROUP : (i + 1) * GROUP, :].rearrange("(p t) c -> p (t c)", t=TILES)
+        first = sum(GROUPS[:i])
+        return dram[first : first + GROUPS[i], :].rearrange("(p t) c -> p (t c)", t=tiles_of(i))
 
     with tc.manual_schedule(), tc.tile_pool(name="consts", bufs=1) as consts, tc.tile_pool(
         name="inputs", bufs=1
@@ -42,33 +47,39 @@ def tile_additivecoupling_pa_t_kernel(tc, x, h_prev, w_hid, b_hid, w_out, b_out,
         hp_tiles = []
         x_tiles = []
         for i in range(N_GROUPS):
-            hp_sb = inputs.tile([P, TILES * MP], BF16, name="hp%d" % i)
+            hp_sb = inputs.tile([P, tiles_of(i) * MP], BF16, name="hp%d" % i)
             hp_tiles.append(hp_sb)
-            x_sb = inputs.tile([P, TILES * D], BF16, name="x%d" % i)
+            x_sb = inputs.tile([P, tiles_of(i) * D], BF16, name="x%d" % i)
             x_tiles.append(x_sb)
-        nc.sync.dma_start(out=hp_tiles[0][:], in_=token_rows(h_prev, 0))
-        whid_raw = consts.tile([P, PACK, MID], BF16)
+        whid_raw = []
         for g in range(MID_PASSES):
-            cols = slice(g * K_PASS, (g + 1) * K_PASS)
+            whid_half = consts.tile([P, PACK, K_PASS], BF16, name="whid_raw%d" % g)
+            whid_raw.append(whid_half)
             nc.sync.dma_start(
-                out=whid_raw[:, :, cols], in_=w_hid[:, cols].rearrange("(q j) n -> q j n", j=PACK)
+                out=whid_half[:],
+                in_=w_hid[:, g * K_PASS : (g + 1) * K_PASS].rearrange("(q j) n -> q j n", j=PACK),
             )
+            if g == 0:
+                nc.sync.dma_start(out=hp_tiles[0][:], in_=token_rows(h_prev, 0))
         nc.sync.dma_start(out=hp_tiles[1][:], in_=token_rows(h_prev, 1))
         wout_raw = consts.tile([P, MID_PASSES, PACK, HALF], BF16)
         nc.sync.dma_start(
             out=wout_raw[:], in_=w_out.rearrange("(g p j) n -> p g j n", g=MID_PASSES, j=PACK)
         )
         bout = consts.tile([P, HALF], BF16)
-        for i in range(N_GROUPS):
+        nc.sync.dma_start(out=bout[:], in_=b_out.partition_broadcast(P))
+
+        def load_group(i):
+            nc.sync.dma_start(out=x_tiles[i][:], in_=token_rows(x, i))
             if i + 2 < N_GROUPS:
                 nc.sync.dma_start(out=hp_tiles[i + 2][:], in_=token_rows(h_prev, i + 2))
-            nc.sync.dma_start(out=x_tiles[i][:], in_=token_rows(x, i))
-            if i == 0:
-                nc.sync.dma_start(out=bout[:], in_=b_out.partition_broadcast(P))
 
-        bhid_bf = consts.tile([P, MID_PASSES * PACK], BF16)
+        for i in range(2):
+            load_group(i)
+
+        bhid = consts.tile([P, MID_PASSES * PACK], BF16)
         nc.scalar.dma_start(
-            out=bhid_bf[:].rearrange("p (g j) -> p g j", j=PACK),
+            out=bhid[:].rearrange("p (g j) -> p g j", j=PACK),
             in_=b_hid.rearrange("(g p j) -> p g j", g=MID_PASSES, j=PACK),
         )
 
@@ -77,11 +88,9 @@ def tile_additivecoupling_pa_t_kernel(tc, x, h_prev, w_hid, b_hid, w_out, b_out,
 
         shift_planes = []
         for s in range(2):
-            planes_sb = consts.tile([P, TILES, 2, HALF], F32, name="shift_planes%d" % s)
-            nc.vector.memset(planes_sb[:, :, 0, :], 0.0)
+            planes_sb = consts.tile([P, MAX_TILES, 2, HALF], F32, name="shift_planes%d" % s)
+            nc.gpsimd.memset(planes_sb[:, :, 0, :], 0.0)
             shift_planes.append(planes_sb)
-        bhid = consts.tile([P, MID_PASSES * PACK], F32)
-        nc.vector.tensor_copy(out=bhid[:], in_=bhid_bf[:])
 
         whid_grouped = consts.tile([P, MID, PACK], BF16, align_bytes=64)
         whid_codes = consts.tile([P, MID], U32, align_bytes=64)
@@ -90,23 +99,28 @@ def tile_additivecoupling_pa_t_kernel(tc, x, h_prev, w_hid, b_hid, w_out, b_out,
         wout_codes = consts.tile([P, MID_PASSES, HALF], U32, align_bytes=64)
         wout_scales = consts.tile([P, MID_PASSES, HALF], U8, align_bytes=64)
 
+        def regroup_w_hid(g, half):
+            cols = slice(g * K_PASS, (g + 1) * K_PASS)
+            j2 = slice(2 * half, 2 * half + 2)
+            nc.vector.tensor_copy(
+                out=whid_grouped[:, cols, :].rearrange("q (j p) s -> q j p s", j=PACK)[:, j2],
+                in_=whid_raw[g][:].rearrange("q s (p j) -> q j p s", j=PACK)[:, j2],
+            )
+
         def quantise_w_hid(g):
             cols = slice(g * K_PASS, (g + 1) * K_PASS)
-            nc.vector.tensor_copy(
-                out=whid_grouped[:, cols, :].rearrange("q (j p) s -> q j p s", j=PACK),
-                in_=whid_raw[:, :, cols].rearrange("q s (p j) -> q j p s", j=PACK),
-            )
             nc.vector.quantize_mx(
                 out=whid_codes[:, cols].bitcast(FP8X4),
                 scales=whid_scales[:, cols],
                 in_=whid_grouped[:, cols, :].rearrange("q c s -> q (c s)"),
             )
 
+        def regroup_w_out(g):
+            nc.vector.tensor_copy(
+                out=wout_grouped[:, g], in_=wout_raw[:, g].rearrange("p j n -> p n j")
+            )
+
         def quantise_w_out():
-            for g in range(MID_PASSES):
-                nc.vector.tensor_copy(
-                    out=wout_grouped[:, g], in_=wout_raw[:, g].rearrange("p j n -> p n j")
-                )
             for g in range(MID_PASSES):
                 for n0, n1 in OUT_PIECES:
                     nc.vector.quantize_mx(
@@ -126,7 +140,7 @@ def tile_additivecoupling_pa_t_kernel(tc, x, h_prev, w_hid, b_hid, w_out, b_out,
 
         def transpose_h_prev(i):
             hp_words = hp_tiles[i][:].bitcast(F32)
-            for b in range(TILES // 2):
+            for b in range(tiles_of(i) // 2):
                 flipped[i, b] = psum_t.tile([P, 2, 2 * P], F32, name="flipped")
                 for t2 in range(2):
                     for u in range(2):
@@ -139,64 +153,75 @@ def tile_additivecoupling_pa_t_kernel(tc, x, h_prev, w_hid, b_hid, w_out, b_out,
 
         def copy_h_prev(i):
             hp_grouped[i] = work.tile(
-                [P, GROUP * PACK], BF16, align_bytes=64, bufs=2, name="hp_grouped"
+                [P, MAX_GROUP * PACK], BF16, align_bytes=64, bufs=2, name="hp_grouped"
             )
             grouped_words = hp_grouped[i][:].bitcast(F32).rearrange("q (c u) -> q c u", u=2)
-            for b in range(TILES // 2):
+            for b in range(tiles_of(i) // 2):
                 nc.scalar.copy(
                     out=grouped_words[:, b * 2 * P : (b + 1) * 2 * P, :],
                     in_=flipped[i, b][:].rearrange("q u c -> q c u"),
                 )
 
         def quantise_h_prev(i):
-            hp_codes = work.tile([P, GROUP], U32, align_bytes=64)
-            hp_scales = work.tile([P, GROUP], U8, align_bytes=64)
+            n = GROUPS[i]
+            hp_codes = work.tile([P, MAX_GROUP], U32, align_bytes=64)
+            hp_scales = work.tile([P, MAX_GROUP], U8, align_bytes=64)
             nc.vector.quantize_mx(
-                out=hp_codes[:].bitcast(FP8X4), scales=hp_scales[:], in_=hp_grouped[i][:]
+                out=hp_codes[:, :n].bitcast(FP8X4),
+                scales=hp_scales[:, :n],
+                in_=hp_grouped[i][:, : n * PACK],
             )
             hp_mx[i] = (hp_codes, hp_scales)
 
         def hidden_matmuls(i, g):
             hp_codes, hp_scales = hp_mx[i]
+            n = GROUPS[i]
             for j in range(PACK):
                 m = g * PACK + j
-                h_acc[i, g, j] = psum_h.tile([P, GROUP], F32, name="h_acc")
+                h_acc[i, g, j] = psum_h.tile([P, MAX_GROUP], F32, name="h_acc")
                 nc.tensor.matmul_mx(
-                    out=h_acc[i, g, j][:],
+                    out=h_acc[i, g, j][:, :n],
                     lhsT=whid_codes[:, m * P : (m + 1) * P].bitcast(FP8X4),
                     lhsT_scale=whid_scales[:, m * P : (m + 1) * P],
-                    rhs=hp_codes[:].bitcast(FP8X4),
-                    rhs_scale=hp_scales[:],
+                    rhs=hp_codes[:, :n].bitcast(FP8X4),
+                    rhs_scale=hp_scales[:, :n],
                     start=True,
                     stop=True,
                 )
 
         def hidden_relu(i, g):
-            h_rows[i, g] = work.tile([P, PACK, GROUP], BF16, name="h_rows")
+            n = GROUPS[i]
+            h_rows[i, g] = work.tile([P, PACK, MAX_GROUP], BF16, name="h_rows")
             for j in range(PACK):
                 m = g * PACK + j
                 nc.scalar.activation(
-                    out=h_rows[i, g][:, j, :], in_=h_acc[i, g, j][:], func=RELU, bias=bhid[:, m : m + 1]
+                    out=h_rows[i, g][:, j, :n],
+                    in_=h_acc[i, g, j][:, :n],
+                    func=RELU,
+                    bias=bhid[:, m : m + 1],
                 )
 
         def regroup_h(i, g):
-            copy = nc.scalar.copy if (g == 1 and i > 0) else nc.vector.tensor_copy
-            h_grouped[i, g] = work.tile([P, GROUP, PACK], BF16, align_bytes=64, name="h_grouped")
+            n = GROUPS[i]
+            on_scalar = (g == 1 and i >= 2) or i >= N_GROUPS - 2
+            copy = nc.scalar.copy if on_scalar else nc.vector.tensor_copy
+            h_grouped[i, g] = work.tile([P, MAX_GROUP, PACK], BF16, align_bytes=64, name="h_grouped")
             copy(
-                out=h_grouped[i, g][:].rearrange("p (c i) j -> p c j i", i=4),
-                in_=h_rows[i, g][:].rearrange("p j (c i) -> p c j i", i=4),
+                out=h_grouped[i, g][:, :n].rearrange("p (c i) j -> p c j i", i=4),
+                in_=h_rows[i, g][:, :, :n].rearrange("p j (c i) -> p c j i", i=4),
             )
 
         def quantise_h(i, g):
+            n = GROUPS[i]
             if g == 0:
-                h_codes = work.tile([P, MID_PASSES, GROUP], U32, align_bytes=64)
-                h_scales = work.tile([P, MID_PASSES, GROUP], U8, align_bytes=64)
+                h_codes = work.tile([P, MID_PASSES, MAX_GROUP], U32, align_bytes=64)
+                h_scales = work.tile([P, MID_PASSES, MAX_GROUP], U8, align_bytes=64)
                 h_mx[i] = (h_codes, h_scales)
             h_codes, h_scales = h_mx[i]
             nc.vector.quantize_mx(
-                out=h_codes[:, g, :].bitcast(FP8X4),
-                scales=h_scales[:, g, :],
-                in_=h_grouped[i, g][:].rearrange("p c j -> p (c j)"),
+                out=h_codes[:, g, :n].bitcast(FP8X4),
+                scales=h_scales[:, g, :n],
+                in_=h_grouped[i, g][:, :n].rearrange("p c j -> p (c j)"),
             )
 
         def shift_matmuls(i, pair):
@@ -223,45 +248,66 @@ def tile_additivecoupling_pa_t_kernel(tc, x, h_prev, w_hid, b_hid, w_out, b_out,
                 )
 
         def add_to_x(i, pair):
-            tiles = slice(2 * pair, 2 * pair + 2)
             y_sb = work.tile([P, 2, HALF, 2], F32)
-            nc.vector.tensor_tensor(
-                out=y_sb[:],
-                in0=x_tiles[i][:].rearrange("p (t c e) -> p t c e", t=TILES, e=2)[:, tiles],
-                in1=shift_planes[i % 2][:, tiles].rearrange("p t e c -> p t c e"),
-                op=ADD,
-            )
-            nc.sync.dma_start(
-                out=token_rows(out, i).rearrange("p (t c) -> p t c", t=TILES)[:, tiles],
-                in_=y_sb[:].rearrange("p t c e -> p t (c e)"),
-            )
+            step = 1 if i == N_GROUPS - 1 else 2
+            for k in range(0, 2, step):
+                tiles = slice(2 * pair + k, 2 * pair + k + step)
+                nc.vector.tensor_tensor(
+                    out=y_sb[:, k : k + step],
+                    in0=x_tiles[i][:].rearrange("p (t c e) -> p t c e", t=tiles_of(i), e=2)[:, tiles],
+                    in1=shift_planes[i % 2][:, tiles].rearrange("p t e c -> p t c e"),
+                    op=ADD,
+                )
+                nc.sync.dma_start(
+                    out=token_rows(out, i).rearrange("p (t c) -> p t c", t=tiles_of(i))[:, tiles],
+                    in_=y_sb[:, k : k + step].rearrange("p t c e -> p t (c e)"),
+                )
 
-        def run(step, i, *args):
-            if 0 <= i < N_GROUPS:
-                step(i, *args)
+        def run(step, i, arg=None):
+            if not 0 <= i < N_GROUPS:
+                return
+            if step in (shift_matmuls, add_b_out, add_to_x) and 2 * arg >= tiles_of(i):
+                return
+            if arg is None:
+                step(i)
+            else:
+                step(i, arg)
 
         transpose_h_prev(0)
         copy_h_prev(0)
+        regroup_w_hid(0, 0)
+        regroup_w_hid(0, 1)
         quantise_w_hid(0)
+        regroup_w_hid(1, 0)
         quantise_h_prev(0)
         hidden_matmuls(0, 0)
+        transpose_h_prev(1)
+        regroup_w_hid(1, 1)
         quantise_w_hid(1)
-        quantise_w_out()
         for i in range(N_GROUPS + LAG):
+            run(load_group, i + 2)
             run(quantise_h, i - 1, 1)
-            run(transpose_h_prev, i + 1)
-            run(shift_matmuls, i - 1, 0)
             run(hidden_relu, i, 0)
-            run(add_to_x, i - 2, 1)
-            run(add_b_out, i - 1, 0)
             run(hidden_matmuls, i, 1)
-            run(copy_h_prev, i + 1)
+            if i == 0:
+                copy_h_prev(1)
+                transpose_h_prev(2)
+            run(shift_matmuls, i - 1, 0)
+            run(add_to_x, i - 2, 1)
+            run(hidden_relu, i, 1)
             run(regroup_h, i, 0)
+            if i == 0:
+                regroup_w_out(0)
             run(quantise_h_prev, i + 1)
+            run(hidden_matmuls, i + 1, 0)
+            run(add_b_out, i - 1, 0)
+            run(copy_h_prev, i + 2)
             run(quantise_h, i, 0)
             run(shift_matmuls, i - 1, 1)
-            run(hidden_relu, i, 1)
-            run(hidden_matmuls, i + 1, 0)
-            run(add_b_out, i - 1, 1)
+            run(transpose_h_prev, i + 3)
             run(add_to_x, i - 1, 0)
             run(regroup_h, i, 1)
+            if i == 0:
+                regroup_w_out(1)
+                quantise_w_out()
+            run(add_b_out, i - 1, 1)

@@ -22,6 +22,8 @@ N_GROUPS = len(GROUPS)
 MID_PASSES = MID // K_PASS
 OUT_PIECES = ((0, 256), (256, 384))
 
+GPSIMD_COLS = 96
+
 LAG = 2
 
 FLOPS = 2 * TOKENS * (MP * MID + MID * HALF)
@@ -203,13 +205,20 @@ def tile_additivecoupling_pa_t_kernel(tc, x, h_prev, w_hid, b_hid, w_out, b_out,
 
         def regroup_h(i, g):
             n = GROUPS[i]
-            on_scalar = (g == 1 and i >= 2) or i >= N_GROUPS - 2
-            copy = nc.scalar.copy if on_scalar else nc.vector.tensor_copy
+            if g == 1:
+                scalar_tokens = 0 if i < 2 else n if i >= 7 else 384
+            else:
+                scalar_tokens = n if i >= 7 else 0
             h_grouped[i, g] = work.tile([P, MAX_GROUP, PACK], BF16, align_bytes=64, name="h_grouped")
-            copy(
-                out=h_grouped[i, g][:, :n].rearrange("p (c i) j -> p c j i", i=4),
-                in_=h_rows[i, g][:, :, :n].rearrange("p j (c i) -> p c j i", i=4),
-            )
+            for copy, tokens in (
+                (nc.scalar.copy, slice(0, scalar_tokens)),
+                (nc.vector.tensor_copy, slice(scalar_tokens, n)),
+            ):
+                if tokens.start < tokens.stop:
+                    copy(
+                        out=h_grouped[i, g][:, tokens].rearrange("p (c i) j -> p c j i", i=4),
+                        in_=h_rows[i, g][:, :, tokens].rearrange("p j (c i) -> p c j i", i=4),
+                    )
 
         def quantise_h(i, g):
             n = GROUPS[i]
@@ -248,16 +257,22 @@ def tile_additivecoupling_pa_t_kernel(tc, x, h_prev, w_hid, b_hid, w_out, b_out,
                 )
 
         def add_to_x(i, pair):
+            last = i == N_GROUPS - 1
             y_sb = work.tile([P, 2, HALF, 2], F32)
-            step = 1 if i == N_GROUPS - 1 else 2
+            step = 1 if last else 2
+            cut = HALF if last else HALF - GPSIMD_COLS
             for k in range(0, 2, step):
                 tiles = slice(2 * pair + k, 2 * pair + k + step)
-                nc.vector.tensor_tensor(
-                    out=y_sb[:, k : k + step],
-                    in0=x_tiles[i][:].rearrange("p (t c e) -> p t c e", t=tiles_of(i), e=2)[:, tiles],
-                    in1=shift_planes[i % 2][:, tiles].rearrange("p t e c -> p t c e"),
-                    op=ADD,
-                )
+                shares = [(nc.vector, slice(0, cut))]
+                if not last:
+                    shares.append((nc.gpsimd, slice(cut, HALF)))
+                for engine, cols in shares:
+                    engine.tensor_tensor(
+                        out=y_sb[:, k : k + step, cols],
+                        in0=x_tiles[i][:].rearrange("p (t c e) -> p t c e", t=tiles_of(i), e=2)[:, tiles, cols],
+                        in1=shift_planes[i % 2][:, tiles].rearrange("p t e c -> p t c e")[:, :, cols],
+                        op=ADD,
+                    )
                 nc.sync.dma_start(
                     out=token_rows(out, i).rearrange("p (t c) -> p t c", t=tiles_of(i))[:, tiles],
                     in_=y_sb[:, k : k + step].rearrange("p t c e -> p t (c e)"),
@@ -293,13 +308,13 @@ def tile_additivecoupling_pa_t_kernel(tc, x, h_prev, w_hid, b_hid, w_out, b_out,
                 copy_h_prev(1)
                 transpose_h_prev(2)
             run(shift_matmuls, i - 1, 0)
-            run(add_to_x, i - 2, 1)
             run(hidden_relu, i, 1)
             run(regroup_h, i, 0)
             if i == 0:
                 regroup_w_out(0)
             run(quantise_h_prev, i + 1)
             run(hidden_matmuls, i + 1, 0)
+            run(add_to_x, i - 2, 1)
             run(add_b_out, i - 1, 0)
             run(copy_h_prev, i + 2)
             run(quantise_h, i, 0)

@@ -40,19 +40,30 @@ def tile_additivecoupling_pa_t_kernel(tc, x, h_prev, w_hid, b_hid, w_out, b_out,
         return dram[first : first + GROUPS[i], :].rearrange("(p t) c -> p (t c)", t=tiles_of(i))
 
     with tc.manual_schedule(), tc.tile_pool(name="consts", bufs=1) as consts, tc.tile_pool(
-        name="inputs", bufs=1
+        name="inputs", bufs=5
     ) as inputs, tc.tile_pool(name="work", bufs=3) as work, tc.psum_pool(
         name="psum_t", bufs=2
     ) as psum_t, tc.psum_pool(name="psum_h", bufs=4) as psum_h, tc.psum_pool(
         name="psum_s", bufs=2
     ) as psum_s:
-        hp_tiles = []
-        x_tiles = []
-        for i in range(N_GROUPS):
-            hp_sb = inputs.tile([P, tiles_of(i) * MP], BF16, name="hp%d" % i)
-            hp_tiles.append(hp_sb)
-            x_sb = inputs.tile([P, tiles_of(i) * D], BF16, name="x%d" % i)
-            x_tiles.append(x_sb)
+        bout_row = consts.tile([P, HALF], BF16)
+        nc.gpsimd.memset(bout_row[:], 0.0)
+        ones = consts.tile([P, P], BF16)
+        nc.gpsimd.memset(ones[:], 1.0)
+
+        hp_rows = {}
+        x_rows = {}
+
+        def load_h_prev(i):
+            hp_sb = inputs.tile([P, MAX_TILES * MP], BF16, name="hp_sb")
+            hp_rows[i] = hp_sb[:, : tiles_of(i) * MP]
+            nc.sync.dma_start(out=hp_rows[i], in_=token_rows(h_prev, i))
+
+        def load_x(i):
+            x_sb = inputs.tile([P, MAX_TILES * D], BF16, name="x_sb")
+            x_rows[i] = x_sb[:, : tiles_of(i) * D]
+            nc.sync.dma_start(out=x_rows[i], in_=token_rows(x, i))
+
         whid_raw = []
         for g in range(MID_PASSES):
             whid_half = consts.tile([P, PACK, K_PASS], BF16, name="whid_raw%d" % g)
@@ -62,22 +73,18 @@ def tile_additivecoupling_pa_t_kernel(tc, x, h_prev, w_hid, b_hid, w_out, b_out,
                 in_=w_hid[:, g * K_PASS : (g + 1) * K_PASS].rearrange("(q j) n -> q j n", j=PACK),
             )
             if g == 0:
-                nc.sync.dma_start(out=hp_tiles[0][:], in_=token_rows(h_prev, 0))
-        nc.sync.dma_start(out=hp_tiles[1][:], in_=token_rows(h_prev, 1))
+                load_h_prev(0)
+                nc.sync.dma_start(out=bout_row[0:1, :], in_=b_out.rearrange("(o n) -> o n", o=1))
+        load_h_prev(1)
         wout_raw = consts.tile([P, MID_PASSES, PACK, HALF], BF16)
         nc.sync.dma_start(
             out=wout_raw[:], in_=w_out.rearrange("(g p j) n -> p g j n", g=MID_PASSES, j=PACK)
         )
-        bout = consts.tile([P, HALF], BF16)
-        nc.sync.dma_start(out=bout[:], in_=b_out.partition_broadcast(P))
 
-        def load_group(i):
-            nc.sync.dma_start(out=x_tiles[i][:], in_=token_rows(x, i))
-            if i + 2 < N_GROUPS:
-                nc.sync.dma_start(out=hp_tiles[i + 2][:], in_=token_rows(h_prev, i + 2))
-
-        for i in range(2):
-            load_group(i)
+        load_x(0)
+        load_h_prev(2)
+        load_x(1)
+        load_h_prev(3)
 
         bhid = consts.tile([P, MID_PASSES * PACK], BF16)
         nc.scalar.dma_start(
@@ -131,6 +138,13 @@ def tile_additivecoupling_pa_t_kernel(tc, x, h_prev, w_hid, b_hid, w_out, b_out,
                         in_=wout_grouped[:, g, n0:n1, :].rearrange("p n j -> p (n j)"),
                     )
 
+        bout = consts.tile([P, HALF], BF16)
+
+        def spread_b_out():
+            bout_acc = psum_s.tile([P, HALF], F32, name="shift_acc")
+            nc.tensor.matmul(bout_acc[:], lhsT=ones[:], rhs=bout_row[:], start=True, stop=True)
+            nc.vector.tensor_copy(out=bout[:], in_=bout_acc[:])
+
         flipped = {}
         hp_grouped = {}
         hp_mx = {}
@@ -141,7 +155,7 @@ def tile_additivecoupling_pa_t_kernel(tc, x, h_prev, w_hid, b_hid, w_out, b_out,
         shift_acc = {}
 
         def transpose_h_prev(i):
-            hp_words = hp_tiles[i][:].bitcast(F32)
+            hp_words = hp_rows[i].bitcast(F32)
             for b in range(tiles_of(i) // 2):
                 flipped[i, b] = psum_t.tile([P, 2, 2 * P], F32, name="flipped")
                 for t2 in range(2):
@@ -258,7 +272,7 @@ def tile_additivecoupling_pa_t_kernel(tc, x, h_prev, w_hid, b_hid, w_out, b_out,
 
         def add_to_x(i, pair):
             last = i == N_GROUPS - 1
-            y_sb = work.tile([P, 2, HALF, 2], F32)
+            y_sb = work.tile([P, 2, HALF, 2], F32, bufs=6, name="y_sb")
             step = 1 if last else 2
             cut = HALF if last else HALF - GPSIMD_COLS
             for k in range(0, 2, step):
@@ -269,7 +283,7 @@ def tile_additivecoupling_pa_t_kernel(tc, x, h_prev, w_hid, b_hid, w_out, b_out,
                 for engine, cols in shares:
                     engine.tensor_tensor(
                         out=y_sb[:, k : k + step, cols],
-                        in0=x_tiles[i][:].rearrange("p (t c e) -> p t c e", t=tiles_of(i), e=2)[:, tiles, cols],
+                        in0=x_rows[i].rearrange("p (t c e) -> p t c e", t=tiles_of(i), e=2)[:, tiles, cols],
                         in1=shift_planes[i % 2][:, tiles].rearrange("p t e c -> p t c e")[:, :, cols],
                         op=ADD,
                     )
@@ -299,8 +313,10 @@ def tile_additivecoupling_pa_t_kernel(tc, x, h_prev, w_hid, b_hid, w_out, b_out,
         transpose_h_prev(1)
         regroup_w_hid(1, 1)
         quantise_w_hid(1)
+        spread_b_out()
         for i in range(N_GROUPS + LAG):
-            run(load_group, i + 2)
+            run(load_x, i + 2)
+            run(load_h_prev, i + 4)
             run(quantise_h, i - 1, 1)
             run(hidden_relu, i, 0)
             run(hidden_matmuls, i, 1)

@@ -22,7 +22,9 @@ N_GROUPS = len(GROUPS)
 MID_PASSES = MID // K_PASS
 OUT_PIECES = ((0, 256), (256, 384))
 
-GPSIMD_COLS = 96
+GPSIMD_COLS = 80
+
+OVERLAP_COLS = 4
 
 LAG = 2
 
@@ -272,13 +274,14 @@ def tile_additivecoupling_pa_t_kernel(tc, x, h_prev, w_hid, b_hid, w_out, b_out,
 
         def add_to_x(i, pair):
             last = i == N_GROUPS - 1
+            alone = last or (i == N_GROUPS - 2 and pair == 1)
             y_sb = work.tile([P, 2, HALF, 2], F32, bufs=6, name="y_sb")
             step = 1 if last else 2
-            cut = HALF if last else HALF - GPSIMD_COLS
+            cut = HALF - GPSIMD_COLS
             for k in range(0, 2, step):
                 tiles = slice(2 * pair + k, 2 * pair + k + step)
-                shares = [(nc.vector, slice(0, cut))]
-                if not last:
+                shares = [(nc.vector, slice(0, HALF if alone else cut + OVERLAP_COLS))]
+                if not alone:
                     shares.append((nc.gpsimd, slice(cut, HALF)))
                 for engine, cols in shares:
                     engine.tensor_tensor(
@@ -310,10 +313,10 @@ def tile_additivecoupling_pa_t_kernel(tc, x, h_prev, w_hid, b_hid, w_out, b_out,
         regroup_w_hid(1, 0)
         quantise_h_prev(0)
         hidden_matmuls(0, 0)
-        transpose_h_prev(1)
         regroup_w_hid(1, 1)
         quantise_w_hid(1)
         spread_b_out()
+        transpose_h_prev(1)
         for i in range(N_GROUPS + LAG):
             run(load_x, i + 2)
             run(load_h_prev, i + 4)

@@ -22,7 +22,7 @@ N_GROUPS = len(GROUPS)
 MID_PASSES = MID // K_PASS
 OUT_PIECES = ((0, 256), (256, 384))
 
-GPSIMD_COLS = 80
+GPSIMD_COLS = 72
 
 OVERLAP_COLS = 4
 
@@ -70,23 +70,32 @@ def tile_additivecoupling_pa_t_kernel(tc, x, h_prev, w_hid, b_hid, w_out, b_out,
         for g in range(MID_PASSES):
             whid_half = consts.tile([P, PACK, K_PASS], BF16, name="whid_raw%d" % g)
             whid_raw.append(whid_half)
+        wout_raw = consts.tile([P, MID_PASSES, PACK, HALF], BF16)
+
+        def load_w_hid(g):
             nc.sync.dma_start(
-                out=whid_half[:],
+                out=whid_raw[g][:],
                 in_=w_hid[:, g * K_PASS : (g + 1) * K_PASS].rearrange("(q j) n -> q j n", j=PACK),
             )
-            if g == 0:
-                load_h_prev(0)
-                nc.sync.dma_start(out=bout_row[0:1, :], in_=b_out.rearrange("(o n) -> o n", o=1))
-        load_h_prev(1)
-        wout_raw = consts.tile([P, MID_PASSES, PACK, HALF], BF16)
-        nc.sync.dma_start(
-            out=wout_raw[:], in_=w_out.rearrange("(g p j) n -> p g j n", g=MID_PASSES, j=PACK)
-        )
 
-        load_x(0)
+        def load_w_out():
+            nc.sync.dma_start(
+                out=wout_raw[:], in_=w_out.rearrange("(g p j) n -> p g j n", g=MID_PASSES, j=PACK)
+            )
+
+        def load_b_out():
+            nc.sync.dma_start(out=bout_row[0:1, :], in_=b_out.rearrange("(o n) -> o n", o=1))
+
+        load_h_prev(0)
+        load_w_hid(0)
+        load_h_prev(1)
+        load_w_hid(1)
+        load_b_out()
+        load_w_out()
         load_h_prev(2)
-        load_x(1)
         load_h_prev(3)
+        load_x(0)
+        load_x(1)
 
         bhid = consts.tile([P, MID_PASSES * PACK], BF16)
         nc.scalar.dma_start(
@@ -222,7 +231,7 @@ def tile_additivecoupling_pa_t_kernel(tc, x, h_prev, w_hid, b_hid, w_out, b_out,
         def regroup_h(i, g):
             n = GROUPS[i]
             if g == 1:
-                scalar_tokens = 0 if i < 2 else n if i >= 7 else 384
+                scalar_tokens = 0 if i < 2 else n if i >= 7 else 448
             else:
                 scalar_tokens = n if i >= 7 else 0
             h_grouped[i, g] = work.tile([P, MAX_GROUP, PACK], BF16, align_bytes=64, name="h_grouped")
@@ -274,7 +283,7 @@ def tile_additivecoupling_pa_t_kernel(tc, x, h_prev, w_hid, b_hid, w_out, b_out,
 
         def add_to_x(i, pair):
             last = i == N_GROUPS - 1
-            alone = last or (i == N_GROUPS - 2 and pair == 1)
+            alone = last or i == 0 or (i == N_GROUPS - 2 and pair == 1)
             y_sb = work.tile([P, 2, HALF, 2], F32, bufs=6, name="y_sb")
             step = 1 if last else 2
             cut = HALF - GPSIMD_COLS
@@ -309,14 +318,17 @@ def tile_additivecoupling_pa_t_kernel(tc, x, h_prev, w_hid, b_hid, w_out, b_out,
         copy_h_prev(0)
         regroup_w_hid(0, 0)
         regroup_w_hid(0, 1)
-        quantise_w_hid(0)
-        regroup_w_hid(1, 0)
         quantise_h_prev(0)
+        quantise_w_hid(0)
+        transpose_h_prev(1)
+        copy_h_prev(1)
         hidden_matmuls(0, 0)
+        regroup_w_hid(1, 0)
         regroup_w_hid(1, 1)
         quantise_w_hid(1)
+        quantise_h_prev(1)
         spread_b_out()
-        transpose_h_prev(1)
+        regroup_w_out(0)
         for i in range(N_GROUPS + LAG):
             run(load_x, i + 2)
             run(load_h_prev, i + 4)
@@ -324,14 +336,14 @@ def tile_additivecoupling_pa_t_kernel(tc, x, h_prev, w_hid, b_hid, w_out, b_out,
             run(hidden_relu, i, 0)
             run(hidden_matmuls, i, 1)
             if i == 0:
-                copy_h_prev(1)
                 transpose_h_prev(2)
             run(shift_matmuls, i - 1, 0)
             run(hidden_relu, i, 1)
+            if i > 0:
+                run(quantise_h_prev, i + 1)
             run(regroup_h, i, 0)
             if i == 0:
-                regroup_w_out(0)
-            run(quantise_h_prev, i + 1)
+                regroup_w_out(1)
             run(hidden_matmuls, i + 1, 0)
             run(add_to_x, i - 2, 1)
             run(add_b_out, i - 1, 0)
@@ -342,6 +354,5 @@ def tile_additivecoupling_pa_t_kernel(tc, x, h_prev, w_hid, b_hid, w_out, b_out,
             run(add_to_x, i - 1, 0)
             run(regroup_h, i, 1)
             if i == 0:
-                regroup_w_out(1)
                 quantise_w_out()
             run(add_b_out, i - 1, 1)

import concourse.mybir as mybir
from concourse.masks import make_identity

F32 = mybir.dt.float32
BF16 = mybir.dt.bfloat16
U32 = mybir.dt.uint32
U8 = mybir.dt.uint8
FP8X4 = mybir.dt.float8_e4m3fn_x4
ADD = mybir.AluOpType.add
RELU = mybir.ActivationFunctionType.Relu

P = 128
PACK = 4
K_PASS = P * PACK

TOKENS, D, MP, MID = 4096, 768, 512, 1024
HALF = D // 2
MAX_GROUP = 512
MAX_TILES = MAX_GROUP // P
GROUPS = (256,) + 7 * (MAX_GROUP,) + (256,)
N_GROUPS = len(GROUPS)
MID_PASSES = MID // K_PASS
OUT_PIECES = ((0, 256), (256, 384))

GPSIMD_COLS = 72

OVERLAP_COLS = 4

LAG = 2

FLOPS = 2 * TOKENS * (MP * MID + MID * HALF)


def tile_additivecoupling_pa_t_kernel(tc, x, h_prev, w_hid, b_hid, w_out, b_out, out):
    nc = tc.nc

    def tiles_of(i):
        return GROUPS[i] // P

    def token_rows(dram, i):
        first = sum(GROUPS[:i])
        return dram[first : first + GROUPS[i], :].rearrange("(p t) c -> p (t c)", t=tiles_of(i))

    with tc.manual_schedule(), tc.tile_pool(name="consts", bufs=1) as consts, tc.tile_pool(
        name="inputs", bufs=5
    ) as inputs, tc.tile_pool(name="work", bufs=3) as work, tc.psum_pool(
        name="psum_t", bufs=2
    ) as psum_t, tc.psum_pool(name="psum_h", bufs=4) as psum_h, tc.psum_pool(
        name="psum_s", bufs=2
    ) as psum_s:
        bout_row = consts.tile([P, HALF], BF16)
        nc.gpsimd.memset(bout_row[:], 0.0)
        ones = consts.tile([P, P], BF16)
        nc.gpsimd.memset(ones[:], 1.0)

        hp_rows = {}
        x_rows = {}

        def load_h_prev(i):
            hp_sb = inputs.tile([P, MAX_TILES * MP], BF16, name="hp_sb")
            hp_rows[i] = hp_sb[:, : tiles_of(i) * MP]
            nc.sync.dma_start(out=hp_rows[i], in_=token_rows(h_prev, i))

        def load_x(i):
            x_sb = inputs.tile([P, MAX_TILES * D], BF16, name="x_sb")
            x_rows[i] = x_sb[:, : tiles_of(i) * D]
            nc.sync.dma_start(out=x_rows[i], in_=token_rows(x, i))

        whid_raw = []
        for g in range(MID_PASSES):
            whid_half = consts.tile([P, PACK, K_PASS], BF16, name="whid_raw%d" % g)
            whid_raw.append(whid_half)
        wout_raw = consts.tile([P, MID_PASSES, PACK, HALF], BF16)

        def load_w_hid(g):
            nc.sync.dma_start(
                out=whid_raw[g][:],
                in_=w_hid[:, g * K_PASS : (g + 1) * K_PASS].rearrange("(q j) n -> q j n", j=PACK),
            )

        def load_w_out():
            nc.sync.dma_start(
                out=wout_raw[:], in_=w_out.rearrange("(g p j) n -> p g j n", g=MID_PASSES, j=PACK)
            )

        def load_b_out():
            nc.sync.dma_start(out=bout_row[0:1, :], in_=b_out.rearrange("(o n) -> o n", o=1))

        load_h_prev(0)
        load_w_hid(0)
        load_h_prev(1)
        load_w_hid(1)
        load_b_out()
        load_w_out()
        load_h_prev(2)
        load_h_prev(3)
        load_x(0)
        load_x(1)

        bhid = consts.tile([P, MID_PASSES * PACK], BF16)
        nc.scalar.dma_start(
            out=bhid[:].rearrange("p (g j) -> p g j", j=PACK),
            in_=b_hid.rearrange("(g p j) -> p g j", g=MID_PASSES, j=PACK),
        )

        ident = consts.tile([P, P], F32)
        make_identity(nc, ident[:])

        shift_planes = []
        for s in range(2):
            planes_sb = consts.tile([P, MAX_TILES, 2, HALF], F32, name="shift_planes%d" % s)
            nc.gpsimd.memset(planes_sb[:, :, 0, :], 0.0)
            shift_planes.append(planes_sb)

        whid_grouped = consts.tile([P, MID, PACK], BF16, align_bytes=64)
        whid_codes = consts.tile([P, MID], U32, align_bytes=64)
        whid_scales = consts.tile([P, MID], U8, align_bytes=64)
        wout_grouped = consts.tile([P, MID_PASSES, HALF, PACK], BF16, align_bytes=64)
        wout_codes = consts.tile([P, MID_PASSES, HALF], U32, align_bytes=64)
        wout_scales = consts.tile([P, MID_PASSES, HALF], U8, align_bytes=64)

        def regroup_w_hid(g, half):
            cols = slice(g * K_PASS, (g + 1) * K_PASS)
            j2 = slice(2 * half, 2 * half + 2)
            nc.vector.tensor_copy(
                out=whid_grouped[:, cols, :].rearrange("q (j p) s -> q j p s", j=PACK)[:, j2],
                in_=whid_raw[g][:].rearrange("q s (p j) -> q j p s", j=PACK)[:, j2],
            )

        def quantise_w_hid(g):
            cols = slice(g * K_PASS, (g + 1) * K_PASS)
            nc.vector.quantize_mx(
                out=whid_codes[:, cols].bitcast(FP8X4),
                scales=whid_scales[:, cols],
                in_=whid_grouped[:, cols, :].rearrange("q c s -> q (c s)"),
            )

        def regroup_w_out(g):
            nc.vector.tensor_copy(
                out=wout_grouped[:, g], in_=wout_raw[:, g].rearrange("p j n -> p n j")
            )

        def quantise_w_out():
            for g in range(MID_PASSES):
                for n0, n1 in OUT_PIECES:
                    nc.vector.quantize_mx(
                        out=wout_codes[:, g, n0:n1].bitcast(FP8X4),
                        scales=wout_scales[:, g, n0:n1],
                        in_=wout_grouped[:, g, n0:n1, :].rearrange("p n j -> p (n j)"),
                    )

        bout = consts.tile([P, HALF], BF16)

        def spread_b_out():
            bout_acc = psum_s.tile([P, HALF], F32, name="shift_acc")
            nc.tensor.matmul(bout_acc[:], lhsT=ones[:], rhs=bout_row[:], start=True, stop=True)
            nc.vector.tensor_copy(out=bout[:], in_=bout_acc[:])

        flipped = {}
        hp_grouped = {}
        hp_mx = {}
        h_acc = {}
        h_rows = {}
        h_grouped = {}
        h_mx = {}
        shift_acc = {}

        def transpose_h_prev(i):
            hp_words = hp_rows[i].bitcast(F32)
            for b in range(tiles_of(i) // 2):
                flipped[i, b] = psum_t.tile([P, 2, 2 * P], F32, name="flipped")
                for t2 in range(2):
                    for u in range(2):
                        row_words = (2 * b + t2) * 2 * P
                        nc.tensor.transpose(
                            flipped[i, b][:, u, t2 * P : (t2 + 1) * P],
                            hp_words[:, row_words + u : row_words + 2 * P : 2],
                            ident[:],
                        )

        def copy_h_prev(i):
            hp_grouped[i] = work.tile(
                [P, MAX_GROUP * PACK], BF16, align_bytes=64, bufs=2, name="hp_grouped"
            )
            grouped_words = hp_grouped[i][:].bitcast(F32).rearrange("q (c u) -> q c u", u=2)
            for b in range(tiles_of(i) // 2):
                nc.scalar.copy(
                    out=grouped_words[:, b * 2 * P : (b + 1) * 2 * P, :],
                    in_=flipped[i, b][:].rearrange("q u c -> q c u"),
                )

        def quantise_h_prev(i):
            n = GROUPS[i]
            hp_codes = work.tile([P, MAX_GROUP], U32, align_bytes=64)
            hp_scales = work.tile([P, MAX_GROUP], U8, align_bytes=64)
            nc.vector.quantize_mx(
                out=hp_codes[:, :n].bitcast(FP8X4),
                scales=hp_scales[:, :n],
                in_=hp_grouped[i][:, : n * PACK],
            )
            hp_mx[i] = (hp_codes, hp_scales)

        def hidden_matmuls(i, g):
            hp_codes, hp_scales = hp_mx[i]
            n = GROUPS[i]
            for j in range(PACK):
                m = g * PACK + j
                h_acc[i, g, j] = psum_h.tile([P, MAX_GROUP], F32, name="h_acc")
                nc.tensor.matmul_mx(
                    out=h_acc[i, g, j][:, :n],
                    lhsT=whid_codes[:, m * P : (m + 1) * P].bitcast(FP8X4),
                    lhsT_scale=whid_scales[:, m * P : (m + 1) * P],
                    rhs=hp_codes[:, :n].bitcast(FP8X4),
                    rhs_scale=hp_scales[:, :n],
                    start=True,
                    stop=True,
                )

        def hidden_relu(i, g):
            n = GROUPS[i]
            h_rows[i, g] = work.tile([P, PACK, MAX_GROUP], BF16, name="h_rows")
            for j in range(PACK):
                m = g * PACK + j
                nc.scalar.activation(
                    out=h_rows[i, g][:, j, :n],
                    in_=h_acc[i, g, j][:, :n],
                    func=RELU,
                    bias=bhid[:, m : m + 1],
                )

        def regroup_h(i, g):
            n = GROUPS[i]
            if g == 1:
                scalar_tokens = 0 if i < 2 else n if i >= 7 else 448
            else:
                scalar_tokens = n if i >= 7 else 0
            h_grouped[i, g] = work.tile([P, MAX_GROUP, PACK], BF16, align_bytes=64, name="h_grouped")
            for copy, tokens in (
                (nc.scalar.copy, slice(0, scalar_tokens)),
                (nc.vector.tensor_copy, slice(scalar_tokens, n)),
            ):
                if tokens.start < tokens.stop:
                    copy(
                        out=h_grouped[i, g][:, tokens].rearrange("p (c i) j -> p c j i", i=4),
                        in_=h_rows[i, g][:, :, tokens].rearrange("p j (c i) -> p c j i", i=4),
                    )

        def quantise_h(i, g):
            n = GROUPS[i]
            if g == 0:
                h_codes = work.tile([P, MID_PASSES, MAX_GROUP], U32, align_bytes=64)
                h_scales = work.tile([P, MID_PASSES, MAX_GROUP], U8, align_bytes=64)
                h_mx[i] = (h_codes, h_scales)
            h_codes, h_scales = h_mx[i]
            nc.vector.quantize_mx(
                out=h_codes[:, g, :n].bitcast(FP8X4),
                scales=h_scales[:, g, :n],
                in_=h_grouped[i, g][:, :n].rearrange("p c j -> p (c j)"),
            )

        def shift_matmuls(i, pair):
            h_codes, h_scales = h_mx[i]
            for t in (2 * pair, 2 * pair + 1):
                tokens = slice(t * P, (t + 1) * P)
                shift_acc[i, t] = psum_s.tile([P, HALF], F32, name="shift_acc")
                for n0, n1 in OUT_PIECES:
                    for g in range(MID_PASSES):
                        nc.tensor.matmul_mx(
                            out=shift_acc[i, t][:, n0:n1],
                            lhsT=h_codes[:, g, tokens].bitcast(FP8X4),
                            lhsT_scale=h_scales[:, g, tokens],
                            rhs=wout_codes[:, g, n0:n1].bitcast(FP8X4),
                            rhs_scale=wout_scales[:, g, n0:n1],
                            start=(g == 0),
                            stop=(g == MID_PASSES - 1),
                        )

        def add_b_out(i, pair):
            for t in (2 * pair, 2 * pair + 1):
                nc.vector.tensor_tensor(
                    out=shift_planes[i % 2][:, t, 1, :], in0=shift_acc[i, t][:], in1=bout[:], op=ADD
                )

        def add_to_x(i, pair):
            last = i == N_GROUPS - 1
            alone = last or i == 0 or (i == N_GROUPS - 2 and pair == 1)
            y_sb = work.tile([P, 2, HALF, 2], F32, bufs=6, name="y_sb")
            step = 1 if last else 2
            cut = HALF - GPSIMD_COLS
            for k in range(0, 2, step):
                tiles = slice(2 * pair + k, 2 * pair + k + step)
                shares = [(nc.vector, slice(0, HALF if alone else cut + OVERLAP_COLS))]
                if not alone:
                    shares.append((nc.gpsimd, slice(cut, HALF)))
                for engine, cols in shares:
                    engine.tensor_tensor(
                        out=y_sb[:, k : k + step, cols],
                        in0=x_rows[i].rearrange("p (t c e) -> p t c e", t=tiles_of(i), e=2)[:, tiles, cols],
                        in1=shift_planes[i % 2][:, tiles].rearrange("p t e c -> p t c e")[:, :, cols],
                        op=ADD,
                    )
                nc.sync.dma_start(
                    out=token_rows(out, i).rearrange("p (t c) -> p t c", t=tiles_of(i))[:, tiles],
                    in_=y_sb[:, k : k + step].rearrange("p t c e -> p t (c e)"),
                )

        def run(step, i, arg=None):
            if not 0 <= i < N_GROUPS:
                return
            if step in (shift_matmuls, add_b_out, add_to_x) and 2 * arg >= tiles_of(i):
                return
            if arg is None:
                step(i)
            else:
                step(i, arg)

        transpose_h_prev(0)
        copy_h_prev(0)
        regroup_w_hid(0, 0)
        regroup_w_hid(0, 1)
        quantise_h_prev(0)
        quantise_w_hid(0)
        transpose_h_prev(1)
        copy_h_prev(1)
        hidden_matmuls(0, 0)
        regroup_w_hid(1, 0)
        regroup_w_hid(1, 1)
        quantise_w_hid(1)
        quantise_h_prev(1)
        spread_b_out()
        regroup_w_out(0)
        for i in range(N_GROUPS + LAG):
            run(load_x, i + 2)
            run(load_h_prev, i + 4)
            run(quantise_h, i - 1, 1)
            run(hidden_relu, i, 0)
            run(hidden_matmuls, i, 1)
            if i == 0:
                transpose_h_prev(2)
            run(shift_matmuls, i - 1, 0)
            run(hidden_relu, i, 1)
            if i > 0:
                run(quantise_h_prev, i + 1)
            run(regroup_h, i, 0)
            if i == 0:
                regroup_w_out(1)
            run(hidden_matmuls, i + 1, 0)
            run(add_to_x, i - 2, 1)
            run(add_b_out, i - 1, 0)
            run(copy_h_prev, i + 2)
            run(quantise_h, i, 0)
            run(shift_matmuls, i - 1, 1)
            run(transpose_h_prev, i + 3)
            run(add_to_x, i - 1, 0)
            run(regroup_h, i, 1)
            if i == 0:
                quantise_w_out()
            run(add_b_out, i - 1, 1)
